import numpy as np
import ml_dtypes


def mxq(x, axis, fmt="e4m3"):
    dtype, down = {"e4m3": (ml_dtypes.float8_e4m3fn, 7), "e5m2": (ml_dtypes.float8_e5m2, 14)}[fmt]
    v = np.moveaxis(np.asarray(x, np.float32).astype(ml_dtypes.bfloat16).astype(np.float64), axis, -1)
    blocks = v.reshape(v.shape[:-1] + (-1, 32))
    amax = np.abs(blocks).max(-1, keepdims=True)
    byte = np.maximum(np.where(amax > 0, np.frexp(amax)[1] - 1 + 127, 0) - down, 1)
    scale = np.exp2(byte - 127.0)
    codes = (blocks / scale).astype(np.float32).astype(dtype).astype(np.float64)
    return np.moveaxis((codes * scale).reshape(v.shape), -1, axis)


WIDE = False


def mx_kscale(k):
    if not WIDE:
        return np.ones(k)
    levels = np.array([10, -10, 5, -5, 0])
    a = np.random.permutation(np.resize(levels, k // 512 * 4)).reshape(k // 512, 4)
    idx = np.arange(k)
    return np.exp2(a[idx // 512, idx % 128 // 32])


BF16 = ml_dtypes.bfloat16


def bf(x):
    return np.asarray(x, np.float32).astype(BF16)


def f64(x):
    return np.asarray(x).astype(np.float64)


B, EN_MID, DE_MID = 8192, 1024, 512
K1 = EN_MID // 2
K2 = DE_MID // 2


def setup_inputs():
    s = mx_kscale(K1)
    in_data = np.random.standard_normal((B, K1, 2)) * s[None, :, None]
    return {"in_data": bf(in_data.reshape(B, EN_MID)),
            "W": bf(np.random.standard_normal((DE_MID, K1)) / np.sqrt(K1) / s[None, :]),
            "bias": bf(np.random.standard_normal(DE_MID) * 0.25)}


def reference(in_data, W, bias):
    Bsz = in_data.shape[0]
    x_imag = f64(in_data).reshape(Bsz, K1, 2)[:, :, 1]
    tmp = mxq(x_imag, 1, "e4m3") @ mxq(f64(W), 1, "e4m3").T
    act = np.maximum(tmp + f64(bias), 0.0)
    out_r = act[:, :K2] - act[:, K2:]
    out = np.stack([out_r, np.zeros_like(out_r)], axis=2)
    return out.reshape(Bsz, DE_MID, 1)

@@ -1,0 +1,210 @@
+from contextlib import ExitStack
+
+import concourse.mybir as mybir
+from concourse.masks import make_identity
+
+F32 = mybir.dt.float32
+BF16 = mybir.dt.bfloat16
+U32 = mybir.dt.uint32
+U8 = mybir.dt.uint8
+FP8X4 = mybir.dt.float8_e4m3fn_x4
+ALU = mybir.AluOpType
+ACT = mybir.ActivationFunctionType
+
+P = 128
+B = 8192
+K = 512
+N = 512
+HALF = N // 2
+PACK = 4
+FLOPS = 2 * B * K * N
+BYTES = B * K * 2 + N * K * 2 + N * 2 + B * N * 4
+
+GROUPS = [1, 1, 2] + [4] * 14 + [2, 1, 1]
+TMAX = 4
+NX = 6
+NR = 2
+ACC_BANKS = 4
+
+
+def tile_middlelayer_t_kernel(tc, in_data, W, bias, out):
+    nc = tc.nc
+    ng = len(GROUPS)
+    assert sum(GROUPS) * P == B
+    base = [P * sum(GROUPS[:g]) for g in range(ng)]
+
+    with ExitStack() as ctx:
+        ctx.enter_context(tc.manual_schedule())
+        const = ctx.enter_context(tc.tile_pool(name="const", bufs=1))
+        xpool = ctx.enter_context(tc.tile_pool(name="xpool", bufs=NX))
+        gpool = ctx.enter_context(tc.tile_pool(name="gpool", bufs=3))
+        qpool = ctx.enter_context(tc.tile_pool(name="qpool", bufs=3))
+        tpool = ctx.enter_context(tc.tile_pool(name="tpool", bufs=3))
+        opool = ctx.enter_context(tc.tile_pool(name="opool", bufs=4))
+        psum_t = ctx.enter_context(tc.psum_pool(name="psum_t", bufs=4))
+        psum_a = ctx.enter_context(tc.psum_pool(name="psum_a", bufs=ACC_BANKS))
+
+        xs = {}
+        xts = {}
+        grps = {}
+        cods = {}
+        scls = {}
+        accs = {}
+        tss = {}
+
+        def load(g):
+            tg = GROUPS[g]
+            x_sb = xpool.tile([P, tg * 2 * K], BF16, tag="x")
+            rows = in_data[base[g] : base[g] + P * tg, :]
+            nc.scalar.dma_start(out=x_sb[:], in_=rows.rearrange("(p t) c -> p (t c)", t=tg))
+            xs[g] = x_sb
+
+        b_row = const.tile([P, N], BF16)
+        nc.vector.memset(b_row[:], 0.0)
+        nc.sync.dma_start(out=b_row[0:1, :], in_=bias.rearrange("(o n) -> o n", o=1))
+        w_sb = const.tile([P, 4, K], BF16)
+        nc.scalar.dma_start(out=w_sb[:], in_=W.rearrange("(c p) k -> p c k", p=P))
+        for g in range(min(NX, ng)):
+            load(g)
+
+        ones = const.tile([P, P], BF16)
+        nc.vector.memset(ones[:], 1.0)
+        ident_b = const.tile([P, P], BF16)
+        make_identity(nc, ident_b[:])
+        ident_f = const.tile([P, P], F32)
+        make_identity(nc, ident_f[:])
+        r_tiles = [const.tile([P, 2, TMAX * HALF], F32, name="r_plane%d" % i) for i in range(NR)]
+        for r_t in r_tiles:
+            nc.vector.memset(r_t[:, 1, :], 0.0)
+
+        w_grp = const.tile([P, N * PACK], BF16, align_bytes=64)
+        w_codes = const.tile([P, N], U32, align_bytes=64)
+        w_scales = const.tile([P, N], U8, align_bytes=64)
+        for h in range(2):
+            wt = psum_t.tile([P, PACK, 2 * P], BF16, tag="xt")
+            for cc in range(2):
+                for u in range(PACK):
+                    nc.tensor.transpose(
+                        wt[:, u, cc * P : (cc + 1) * P],
+                        w_sb[:, 2 * h + cc, u * P : (u + 1) * P],
+                        ident_b[:],
+                    )
+            dst = w_grp[:, h * 2 * P * PACK : (h + 1) * 2 * P * PACK].rearrange("p (n u) -> p n u", u=PACK)
+            src = wt[:].rearrange("p u n -> p n u")
+            if h == 0:
+                nc.vector.tensor_copy(out=dst, in_=src)
+            else:
+                nc.scalar.copy(out=dst, in_=src)
+        nc.vector.quantize_mx(out=w_codes[:].bitcast(FP8X4), scales=w_scales[:], in_=w_grp[:])
+
+        b_ps = psum_a.tile([P, N], F32, tag="acc")
+        nc.tensor.matmul(out=b_ps[:], lhsT=ones[:], rhs=b_row[:], start=True, stop=True)
+        bias_bc = const.tile([P, N], F32)
+        nc.vector.tensor_copy(out=bias_bc[:], in_=b_ps[:])
+
+        def transposes(g):
+            xw = xs[g][:].bitcast(F32)
+            for t in range(GROUPS[g]):
+                xt = psum_t.tile([P, PACK * P], F32, tag="xt")
+                for u in range(PACK):
+                    nc.tensor.transpose(
+                        xt[:, u * P : (u + 1) * P],
+                        xw[:, t * K + u * P : t * K + (u + 1) * P],
+                        ident_f[:],
+                    )
+                xts[(g, t)] = xt
+
+        def regroup(g):
+            tg = GROUPS[g]
+            grp = gpool.tile([P, tg * P * PACK], BF16, tag="grp", align_bytes=64)
+            for t in range(tg):
+                src = xts[(g, t)][:].bitcast(BF16).rearrange("p (u b e) -> p b u e", u=PACK, b=P, e=2)
+                dst = grp[:, t * P * PACK : (t + 1) * P * PACK].rearrange("p (b u) -> p b u", u=PACK)
+                nc.scalar.copy(out=dst, in_=src[:, :, :, 1])
+            grps[g] = grp
+
+        def quantise(g):
+            tg = GROUPS[g]
+            codes = qpool.tile([P, tg * P], U32, tag="codes", align_bytes=64)
+            scales = qpool.tile([P, tg * P], U8, tag="scales", align_bytes=64)
+            nc.vector.quantize_mx(out=codes[:].bitcast(FP8X4), scales=scales[:], in_=grps[g][:])
+            cods[g] = codes
+            scls[g] = scales
+
+        def multiply(g, t):
+            acc = psum_a.tile([P, N], F32, tag="acc")
+            nc.tensor.matmul_mx(
+                out=acc[:],
+                lhsT=cods[g][:, t * P : (t + 1) * P].bitcast(FP8X4),
+                lhsT_scale=scls[g][:, t * P : (t + 1) * P],
+                rhs=w_codes[:].bitcast(FP8X4),
+                rhs_scale=w_scales[:],
+                start=True,
+                stop=True,
+            )
+            accs[(g, t)] = acc
+
+        def add_bias(g, t):
+            if t == 0:
+                ts_new = tpool.tile([P, GROUPS[g], N], F32, tag="ts")
+                tss[g] = ts_new
+            nc.vector.tensor_tensor(out=tss[g][:, t, :], in0=accs[(g, t)][:], in1=bias_bc[:], op=ALU.add)
+
+        def relu_second(g):
+            v = tss[g][:, :, HALF:N]
+            nc.scalar.activation(out=v, in_=v, func=ACT.Relu)
+
+        def fold(g):
+            tg = GROUPS[g]
+            r_t = r_tiles[g % NR]
+            nc.vector.scalar_tensor_tensor(
+                out=r_t[:, 0, 0 : tg * HALF].rearrange("p (t j) -> p t j", t=tg),
+                in0=tss[g][:, :, 0:HALF],
+                scalar=0.0,
+                in1=tss[g][:, :, HALF:N],
+                op0=ALU.max,
+                op1=ALU.subtract,
+            )
+
+        def interleave_store(g):
+            tg = GROUPS[g]
+            r_t = r_tiles[g % NR]
+            o_t = opool.tile([P, tg * N], F32, tag="o")
+            nc.gpsimd.tensor_scalar(
+                out=o_t[:].rearrange("p (m e) -> p m e", e=2),
+                in0=r_t[:, :, 0 : tg * HALF].rearrange("p e m -> p m e"),
+                scalar1=1.0,
+                scalar2=0.0,
+                op0=ALU.mult,
+                op1=ALU.add,
+            )
+            rows = out[base[g] : base[g] + P * tg, :, :]
+            nc.sync.dma_start(out=rows.rearrange("(p t) c o -> p (t c o)", t=tg), in_=o_t[:])
+
+        for s in range(-2, ng + 1):
+            if 0 <= s + 2 < ng:
+                transposes(s + 2)
+                regroup(s + 2)
+                if s + 2 + NX < ng:
+                    load(s + 2 + NX)
+            na = GROUPS[s] if 0 <= s < ng else 0
+            nm = GROUPS[s + 1] if 0 <= s + 1 < ng else 0
+            a_done = 0
+            m_done = 0
+            while a_done < (na + 1) // 2:
+                add_bias(s, a_done)
+                a_done += 1
+            if nm:
+                quantise(s + 1)
+            while a_done < na or m_done < nm:
+                if m_done < nm and (na - a_done) + m_done < ACC_BANKS:
+                    multiply(s + 1, m_done)
+                    m_done += 1
+                else:
+                    add_bias(s, a_done)
+                    a_done += 1
+            if na:
+                relu_second(s)
+            if 0 <= s - 1 < ng:
+                fold(s - 1)
+                interleave_store(s - 1)

@@ -170,13 +170,19 @@ def tile_middlelayer_t_kernel(tc, in_data, W, bias, out):
             tg = GROUPS[g]
             r_t = r_tiles[g % NR]
             o_t = opool.tile([P, tg * N], F32, tag="o")
-            nc.gpsimd.tensor_scalar(
-                out=o_t[:].rearrange("p (m e) -> p m e", e=2),
-                in0=r_t[:, :, 0 : tg * HALF].rearrange("p e m -> p m e"),
-                scalar1=1.0,
-                scalar2=0.0,
-                op0=ALU.mult,
-                op1=ALU.add,
+            cut = (tg - 1) * HALF
+            if cut:
+                nc.gpsimd.tensor_scalar(
+                    out=o_t[:, 0 : 2 * cut].rearrange("p (m e) -> p m e", e=2),
+                    in0=r_t[:, :, 0:cut].rearrange("p e m -> p m e"),
+                    scalar1=1.0,
+                    scalar2=0.0,
+                    op0=ALU.mult,
+                    op1=ALU.add,
+                )
+            nc.scalar.copy(
+                out=o_t[:, 2 * cut : tg * N].rearrange("p (m e) -> p m e", e=2),
+                in_=r_t[:, :, cut : tg * HALF].rearrange("p e m -> p m e"),
             )
             rows = out[base[g] : base[g] + P * tg, :, :]
             nc.sync.dma_start(out=rows.rearrange("(p t) c o -> p (t c o)", t=tg), in_=o_t[:])
@@ -191,9 +197,6 @@ def tile_middlelayer_t_kernel(tc, in_data, W, bias, out):
             nm = GROUPS[s + 1] if 0 <= s + 1 < ng else 0
             a_done = 0
             m_done = 0
-            while a_done < (na + 1) // 2:
-                add_bias(s, a_done)
-                a_done += 1
             if nm:
                 quantise(s + 1)
             while a_done < na or m_done < nm:

from contextlib import ExitStack

import concourse.mybir as mybir
from concourse.masks import make_identity

F32 = mybir.dt.float32
BF16 = mybir.dt.bfloat16
U32 = mybir.dt.uint32
U8 = mybir.dt.uint8
FP8X4 = mybir.dt.float8_e4m3fn_x4
ALU = mybir.AluOpType
ACT = mybir.ActivationFunctionType

P = 128
B = 8192
K = 512
N = 512
HALF = N // 2
PACK = 4
FLOPS = 2 * B * K * N
BYTES = B * K * 2 + N * K * 2 + N * 2 + B * N * 4

GROUPS = [1, 1, 2] + [4] * 14 + [2, 1, 1]
TMAX = 4
NX = 6
NR = 2
ACC_BANKS = 4


def tile_middlelayer_t_kernel(tc, in_data, W, bias, out):
    nc = tc.nc
    ng = len(GROUPS)
    assert sum(GROUPS) * P == B
    base = [P * sum(GROUPS[:g]) for g in range(ng)]

    with ExitStack() as ctx:
        ctx.enter_context(tc.manual_schedule())
        const = ctx.enter_context(tc.tile_pool(name="const", bufs=1))
        xpool = ctx.enter_context(tc.tile_pool(name="xpool", bufs=NX))
        gpool = ctx.enter_context(tc.tile_pool(name="gpool", bufs=3))
        qpool = ctx.enter_context(tc.tile_pool(name="qpool", bufs=3))
        tpool = ctx.enter_context(tc.tile_pool(name="tpool", bufs=3))
        opool = ctx.enter_context(tc.tile_pool(name="opool", bufs=4))
        psum_t = ctx.enter_context(tc.psum_pool(name="psum_t", bufs=4))
        psum_a = ctx.enter_context(tc.psum_pool(name="psum_a", bufs=ACC_BANKS))

        xs = {}
        xts = {}
        grps = {}
        cods = {}
        scls = {}
        accs = {}
        tss = {}

        def load(g):
            tg = GROUPS[g]
            x_sb = xpool.tile([P, tg * 2 * K], BF16, tag="x")
            rows = in_data[base[g] : base[g] + P * tg, :]
            nc.scalar.dma_start(out=x_sb[:], in_=rows.rearrange("(p t) c -> p (t c)", t=tg))
            xs[g] = x_sb

        b_row = const.tile([P, N], BF16)
        nc.vector.memset(b_row[:], 0.0)
        nc.sync.dma_start(out=b_row[0:1, :], in_=bias.rearrange("(o n) -> o n", o=1))
        w_sb = const.tile([P, 4, K], BF16)
        nc.scalar.dma_start(out=w_sb[:], in_=W.rearrange("(c p) k -> p c k", p=P))
        for g in range(min(NX, ng)):
            load(g)

        ones = const.tile([P, P], BF16)
        nc.vector.memset(ones[:], 1.0)
        ident_b = const.tile([P, P], BF16)
        make_identity(nc, ident_b[:])
        ident_f = const.tile([P, P], F32)
        make_identity(nc, ident_f[:])
        r_tiles = [const.tile([P, 2, TMAX * HALF], F32, name="r_plane%d" % i) for i in range(NR)]
        for r_t in r_tiles:
            nc.vector.memset(r_t[:, 1, :], 0.0)

        w_grp = const.tile([P, N * PACK], BF16, align_bytes=64)
        w_codes = const.tile([P, N], U32, align_bytes=64)
        w_scales = const.tile([P, N], U8, align_bytes=64)
        for h in range(2):
            wt = psum_t.tile([P, PACK, 2 * P], BF16, tag="xt")
            for cc in range(2):
                for u in range(PACK):
                    nc.tensor.transpose(
                        wt[:, u, cc * P : (cc + 1) * P],
                        w_sb[:, 2 * h + cc, u * P : (u + 1) * P],
                        ident_b[:],
                    )
            dst = w_grp[:, h * 2 * P * PACK : (h + 1) * 2 * P * PACK].rearrange("p (n u) -> p n u", u=PACK)
            src = wt[:].rearrange("p u n -> p n u")
            if h == 0:
                nc.vector.tensor_copy(out=dst, in_=src)
            else:
                nc.scalar.copy(out=dst, in_=src)
        nc.vector.quantize_mx(out=w_codes[:].bitcast(FP8X4), scales=w_scales[:], in_=w_grp[:])

        b_ps = psum_a.tile([P, N], F32, tag="acc")
        nc.tensor.matmul(out=b_ps[:], lhsT=ones[:], rhs=b_row[:], start=True, stop=True)
        bias_bc = const.tile([P, N], F32)
        nc.vector.tensor_copy(out=bias_bc[:], in_=b_ps[:])

        def transposes(g):
            xw = xs[g][:].bitcast(F32)
            for t in range(GROUPS[g]):
                xt = psum_t.tile([P, PACK * P], F32, tag="xt")
                for u in range(PACK):
                    nc.tensor.transpose(
                        xt[:, u * P : (u + 1) * P],
                        xw[:, t * K + u * P : t * K + (u + 1) * P],
                        ident_f[:],
                    )
                xts[(g, t)] = xt

        def regroup(g):
            tg = GROUPS[g]
            grp = gpool.tile([P, tg * P * PACK], BF16, tag="grp", align_bytes=64)
            for t in range(tg):
                src = xts[(g, t)][:].bitcast(BF16).rearrange("p (u b e) -> p b u e", u=PACK, b=P, e=2)
                dst = grp[:, t * P * PACK : (t + 1) * P * PACK].rearrange("p (b u) -> p b u", u=PACK)
                nc.scalar.copy(out=dst, in_=src[:, :, :, 1])
            grps[g] = grp

        def quantise(g):
            tg = GROUPS[g]
            codes = qpool.tile([P, tg * P], U32, tag="codes", align_bytes=64)
            scales = qpool.tile([P, tg * P], U8, tag="scales", align_bytes=64)
            nc.vector.quantize_mx(out=codes[:].bitcast(FP8X4), scales=scales[:], in_=grps[g][:])
            cods[g] = codes
            scls[g] = scales

        def multiply(g, t):
            acc = psum_a.tile([P, N], F32, tag="acc")
            nc.tensor.matmul_mx(
                out=acc[:],
                lhsT=cods[g][:, t * P : (t + 1) * P].bitcast(FP8X4),
                lhsT_scale=scls[g][:, t * P : (t + 1) * P],
                rhs=w_codes[:].bitcast(FP8X4),
                rhs_scale=w_scales[:],
                start=True,
                stop=True,
            )
            accs[(g, t)] = acc

        def add_bias(g, t):
            if t == 0:
                ts_new = tpool.tile([P, GROUPS[g], N], F32, tag="ts")
                tss[g] = ts_new
            nc.vector.tensor_tensor(out=tss[g][:, t, :], in0=accs[(g, t)][:], in1=bias_bc[:], op=ALU.add)

        def relu_second(g):
            v = tss[g][:, :, HALF:N]
            nc.scalar.activation(out=v, in_=v, func=ACT.Relu)

        def fold(g):
            tg = GROUPS[g]
            r_t = r_tiles[g % NR]
            nc.vector.scalar_tensor_tensor(
                out=r_t[:, 0, 0 : tg * HALF].rearrange("p (t j) -> p t j", t=tg),
                in0=tss[g][:, :, 0:HALF],
                scalar=0.0,
                in1=tss[g][:, :, HALF:N],
                op0=ALU.max,
                op1=ALU.subtract,
            )

        def interleave_store(g):
            tg = GROUPS[g]
            r_t = r_tiles[g % NR]
            o_t = opool.tile([P, tg * N], F32, tag="o")
            cut = (tg - 1) * HALF
            if cut:
                nc.gpsimd.tensor_scalar(
                    out=o_t[:, 0 : 2 * cut].rearrange("p (m e) -> p m e", e=2),
                    in0=r_t[:, :, 0:cut].rearrange("p e m -> p m e"),
                    scalar1=1.0,
                    scalar2=0.0,
                    op0=ALU.mult,
                    op1=ALU.add,
                )
            nc.scalar.copy(
                out=o_t[:, 2 * cut : tg * N].rearrange("p (m e) -> p m e", e=2),
                in_=r_t[:, :, cut : tg * HALF].rearrange("p e m -> p m e"),
            )
            rows = out[base[g] : base[g] + P * tg, :, :]
            nc.sync.dma_start(out=rows.rearrange("(p t) c o -> p (t c o)", t=tg), in_=o_t[:])

        for s in range(-2, ng + 1):
            if 0 <= s + 2 < ng:
                transposes(s + 2)
                regroup(s + 2)
                if s + 2 + NX < ng:
                    load(s + 2 + NX)
            na = GROUPS[s] if 0 <= s < ng else 0
            nm = GROUPS[s + 1] if 0 <= s + 1 < ng else 0
            a_done = 0
            m_done = 0
            if nm:
                quantise(s + 1)
            while a_done < na or m_done < nm:
                if m_done < nm and (na - a_done) + m_done < ACC_BANKS:
                    multiply(s + 1, m_done)
                    m_done += 1
                else:
                    add_bias(s, a_done)
                    a_done += 1
            if na:
                relu_second(s)
            if 0 <= s - 1 < ng:
                fold(s - 1)
                interleave_store(s - 1)
